import numpy as np
import ml_dtypes


def mxq(x, axis, fmt="e4m3"):
    dtype, down = {"e4m3": (ml_dtypes.float8_e4m3fn, 7), "e5m2": (ml_dtypes.float8_e5m2, 14)}[fmt]
    v = np.moveaxis(np.asarray(x, np.float32).astype(ml_dtypes.bfloat16).astype(np.float64), axis, -1)
    blocks = v.reshape(v.shape[:-1] + (-1, 32))
    amax = np.abs(blocks).max(-1, keepdims=True)
    byte = np.maximum(np.where(amax > 0, np.frexp(amax)[1] - 1 + 127, 0) - down, 1)
    scale = np.exp2(byte - 127.0)
    codes = (blocks / scale).astype(np.float32).astype(dtype).astype(np.float64)
    return np.moveaxis((codes * scale).reshape(v.shape), -1, axis)


WIDE = False


def mx_kscale(k):
    if not WIDE:
        return np.ones(k)
    levels = np.array([30, -30])
    if k % 512:
        return np.exp2(np.random.permutation(np.resize(levels, k // 32))).repeat(32)
    a = np.empty((k // 512, 16))
    for p in range(k // 512):
        a[p, :8] = np.random.permutation(np.resize(levels, 8))
        for g in range(8):
            far = levels[np.abs(levels - a[p, g]) >= 10]
            a[p, g + 8] = far[np.random.randint(len(far))]
    return np.exp2(a.ravel()).repeat(32)


BF16 = ml_dtypes.bfloat16


def bf(x):
    return np.asarray(x, np.float32).astype(BF16)


def f64(x):
    return np.asarray(x).astype(np.float64)


NI, NJ, NK, CZ, CM = 512, 512, 512, 128, 16
EPS = 1e-5


def setup_inputs():
    s = mx_kscale(NK)[None, :, None]
    a = 1.2 / NK ** 0.25
    return {"left": bf(np.random.standard_normal((NI, NK, CM)) * a * s),
            "right": bf(np.random.standard_normal((NJ, NK, CM)) * a / s),
            "ln_c_w": bf(1.0 + 0.1 * np.random.standard_normal(CM)),
            "ln_c_b": bf(0.1 * np.random.standard_normal(CM))}


def reference(left, right, ln_c_w, ln_c_b):
    lq = mxq(f64(left).transpose(2, 0, 1), 2, "e5m2")
    rq = mxq(f64(right).transpose(2, 1, 0), 1, "e4m3")
    t = (lq @ rq).transpose(1, 2, 0)
    mu = t.mean(-1, keepdims=True)
    var = t.var(-1, keepdims=True)
    return (t - mu) * (1.0 / np.sqrt(var + EPS)) * f64(ln_c_w) + f64(ln_c_b)

@@ -1,0 +1,258 @@
+from contextlib import ExitStack
+
+import concourse.mybir as mybir
+from concourse.masks import make_identity
+
+NI, NJ, NK, CM = 512, 512, 512, 16
+EPS = 1e-5
+FLOPS = 2 * NI * NJ * NK * CM
+
+F32 = mybir.dt.float32
+BF16 = mybir.dt.bfloat16
+U32 = mybir.dt.uint32
+U8 = mybir.dt.uint8
+E5M2 = mybir.dt.float8_e5m2_x4
+E4M3 = mybir.dt.float8_e4m3fn_x4
+ALU = mybir.AluOpType
+ACT = mybir.ActivationFunctionType
+
+P = 128
+HALF = 64
+CG = 4
+GROUPS = CM // CG
+RAW_BUFS = 6
+LAG = 2
+VECTOR_COLS_LATE = 16
+VECTOR_COLS_LAST = 64
+
+
+def tile_trianglemultiplication_pa_kernel(tc, left, right, ln_c_w, ln_c_b, out):
+    nc = tc.nc
+    tiles = NI // P
+
+    chunks = [("left", 0), ("right", 0)]
+    units = [(0, 0)]
+    first_unit = {}
+    for s in range(1, tiles):
+        chunks.append(("right", s))
+        first_unit[("right", s)] = len(units)
+        units.extend((a, s) for a in range(s))
+        chunks.append(("left", s))
+        first_unit[("left", s)] = len(units)
+        units.extend((s, b) for b in range(s + 1))
+    halves = [(chunk, h) for chunk in chunks for h in range(2)]
+    fills = [(chunk, h, g) for chunk, h in halves for g in range(GROUPS)]
+    per_chunk = 2 * GROUPS
+
+    fills_by = {}
+    start = 0
+    for n_chunk in range(2, len(chunks)):
+        end = first_unit[chunks[n_chunk]]
+        for n in range(start, end):
+            fills_by[n] = n_chunk * per_chunk + -(-per_chunk * (n + 1 - start) // (end - start))
+        start = end
+    last_fill_period = start - 1
+
+    with ExitStack() as ctx:
+        keep = ctx.enter_context(tc.tile_pool(name="keep", bufs=1))
+        work = ctx.enter_context(tc.tile_pool(name="work", bufs=2))
+        psum = ctx.enter_context(tc.psum_pool(name="psum", bufs=1))
+        ctx.enter_context(tc.manual_schedule())
+
+        ident_bf = keep.tile([P, P], BF16, name="ident_bf")
+        ident_f32 = keep.tile([P, P], F32, name="ident_f32")
+        make_identity(nc, ident_bf[:])
+        make_identity(nc, ident_f32[:])
+        gain_bf = keep.tile([P, CM], BF16, name="gain_bf")
+        bias_bf = keep.tile([P, CM], BF16, name="bias_bf")
+        gain = keep.tile([P, CM], F32, name="gain")
+        bias = keep.tile([P, CM], F32, name="bias")
+
+        codes, scales = {}, {}
+        for side, s in chunks:
+            codes[side, s] = keep.tile([P, CM * P], U32, name="codes_%s%d" % (side, s), align_bytes=64)
+            scales[side, s] = keep.tile([P, CM * P], U8, name="scales_%s%d" % (side, s), align_bytes=64)
+
+        raw, grouped = {}, {}
+        t_banks, mean, centred, squares, rstd_t, rstd_bank, result = {}, {}, {}, {}, {}, {}, {}
+
+        def load(n_half):
+            (side, s), h = halves[n_half]
+            src = left if side == "left" else right
+            row0 = s * P + h * HALF
+            rows = src[row0 : row0 + HALF].rearrange("i (g e r) c -> e i g (r c)", e=2, r=16)
+            tile = work.tile([P, NK * CM // 2], BF16, name="raw", bufs=RAW_BUFS)
+            raw[n_half] = tile
+            for e in range(2):
+                nc.sync.dma_start(out=tile[e:P:2, :].rearrange("p (g r) -> p g r", r=16 * CM), in_=rows[e])
+
+        def fill(n_fill):
+            chunk, h, g = fills[n_fill]
+            n_half = n_fill // GROUPS
+            bank = psum.tile([P, CG * 2 * P], BF16, name="turned", tag="aux", bufs=3)
+            for c in range(CG):
+                for u in range(2):
+                    first = CM * u + CG * g + c
+                    slot = 2 * c + u
+                    nc.tensor.transpose(
+                        bank[:, slot * P : (slot + 1) * P], raw[n_half][:, first : NK * CM // 2 : 2 * CM], ident_bf[:]
+                    )
+            if h == 0:
+                grouped[chunk, g] = work.tile([P, CG * P * 4], BF16, name="grouped", bufs=5, align_bytes=64)
+            words = grouped[chunk, g][:].bitcast(F32).rearrange("p (c m u) -> p c m u", c=CG, u=2)
+            nc.scalar.copy(
+                out=words[:, :, h * HALF : (h + 1) * HALF, :],
+                in_=bank[:].bitcast(F32).rearrange("p (c u m) -> p c m u", c=CG, u=2),
+            )
+            if g == GROUPS - 1 and n_half + RAW_BUFS < len(halves):
+                load(n_half + RAW_BUFS)
+
+        def quantize(n_fill):
+            chunk, h, g = fills[n_fill]
+            if h == 1:
+                cols = slice(g * CG * P, (g + 1) * CG * P)
+                nc.vector.quantize_mx(
+                    out=codes[chunk][:, cols].bitcast(E5M2 if chunk[0] == "left" else E4M3),
+                    scales=scales[chunk][:, cols],
+                    in_=grouped[chunk, g][:],
+                )
+
+        def product(n, c, dst, start, stop):
+            a, b = units[n]
+            cols = slice(c * P, (c + 1) * P)
+            nc.tensor.matmul_mx(
+                out=dst,
+                lhsT=codes["left", a][:, cols].bitcast(E5M2),
+                lhsT_scale=scales["left", a][:, cols],
+                rhs=codes["right", b][:, cols].bitcast(E4M3),
+                rhs_scale=scales["right", b][:, cols],
+                start=start,
+                stop=stop,
+            )
+
+        def channel_sum(n):
+            total = psum.tile([P, P], F32, name="total", tag="aux", bufs=3)
+            for c in range(CM):
+                product(n, c, total[:], c == 0, c == CM - 1)
+            return total
+
+        def take_mean(n, total):
+            mean[n] = work.tile([P, P], F32, name="mean")
+            nc.scalar.activation(out=mean[n][:], in_=total[:], func=ACT.Copy, scale=1.0 / CM)
+
+        def products(n):
+            for g in range(GROUPS):
+                bank = psum.tile([P, CG, P], F32, name="t_bank", bufs=GROUPS)
+                t_banks[n, g] = bank
+                for c in range(CG):
+                    product(n, CG * g + c, bank[:, c, :], True, True)
+
+        def centre(n):
+            centred[n] = work.tile([P, CM, P], F32, name="centred", bufs=LAG + 2)
+            mu = mean[n][:].unsqueeze(1).to_broadcast([P, CG, P])
+            for g in range(GROUPS):
+                nc.vector.tensor_tensor(
+                    out=centred[n][:, CG * g : CG * (g + 1), :], in0=t_banks[n, g][:], in1=mu, op=ALU.subtract
+                )
+
+        def square(n, part):
+            if part == 0:
+                squares[n] = work.tile([P, CM, P], F32, name="squares")
+            cs = slice(part * CM // 2, (part + 1) * CM // 2)
+            nc.scalar.activation(out=squares[n][:, cs, :], in_=centred[n][:, cs, :], func=ACT.Square)
+
+        def variance(n):
+            sums = psum.tile([P, P], F32, name="sums", tag="aux", bufs=3)
+            for c in range(CM):
+                nc.tensor.matmul(
+                    sums[:], lhsT=squares[n][:, c, :], rhs=ident_f32[:], start=c == 0, stop=c == CM - 1, is_transpose=True
+                )
+            rstd_t[n] = work.tile([P, P], F32, name="rstd_t")
+            nc.scalar.activation(out=rstd_t[n][:], in_=sums[:], func=ACT.Abs_reciprocal_sqrt, scale=1.0 / CM, bias=EPS)
+
+        def vector_cols(n):
+            if n >= len(units) - LAG:
+                return VECTOR_COLS_LAST
+            return VECTOR_COLS_LATE if n + LAG > last_fill_period else 0
+
+        def turn_rstd(n):
+            bank = psum.tile([P, P + CM], F32, name="rstd_bank")
+            rstd_bank[n] = bank
+            nc.tensor.transpose(bank[:, 0:P], rstd_t[n][:], ident_f32[:])
+            if vector_cols(n):
+                nc.tensor.matmul(bank[:, P : P + CM], lhsT=ident_bf[:], rhs=bias_bf[:], start=True, stop=True)
+
+        def add_bias(engine, n, g, j0, j1, row):
+            cs = slice(CG * g, CG * (g + 1))
+            engine.tensor_tensor(
+                out=result[n][:, j0:j1, cs],
+                in0=centred[n][:, cs, j0:j1].rearrange("p c j -> p j c"),
+                in1=row[:, cs].unsqueeze(1).to_broadcast([P, j1 - j0, CG]),
+                op=ALU.add,
+            )
+
+        def normalise(n):
+            result[n] = work.tile([P, P, CM], F32, name="result", bufs=3)
+            split = P - vector_cols(n)
+            for g in range(GROUPS):
+                for c in range(CG * g, CG * (g + 1)):
+                    nc.vector.scalar_tensor_tensor(
+                        out=centred[n][:, c, :],
+                        in0=centred[n][:, c, :],
+                        scalar=gain[:, c : c + 1],
+                        in1=rstd_bank[n][:, 0:P],
+                        op0=ALU.mult,
+                        op1=ALU.mult,
+                    )
+                add_bias(nc.gpsimd, n, g, 0, split, bias)
+            if split < P:
+                for g in range(GROUPS):
+                    add_bias(nc.vector, n, g, split, P, rstd_bank[n][:, P : P + CM])
+
+        def store(n):
+            a, b = units[n]
+            nc.sync.dma_start(out=out[a * P : (a + 1) * P, b * P : (b + 1) * P, :], in_=result[n][:])
+
+        for n_half in range(RAW_BUFS):
+            load(n_half)
+        nc.sync.dma_start(out=gain_bf[:], in_=ln_c_w.partition_broadcast(P))
+        nc.sync.dma_start(out=bias_bf[:], in_=ln_c_b.partition_broadcast(P))
+
+        done = 2 * per_chunk
+        for n_fill in range(done):
+            fill(n_fill)
+            quantize(n_fill)
+        nc.vector.tensor_copy(out=gain[:], in_=gain_bf[:])
+        nc.vector.tensor_copy(out=bias[:], in_=bias_bf[:])
+        total = channel_sum(0)
+        take_mean(0, total)
+        products(0)
+
+        count = len(units)
+        for n in range(count + LAG):
+            if n >= LAG:
+                turn_rstd(n - LAG)
+            if n < count:
+                centre(n)
+            todo = range(done, fills_by.get(n, done))
+            for n_fill in todo:
+                fill(n_fill)
+            for n_fill in todo:
+                quantize(n_fill)
+            done += len(todo)
+            if 1 <= n <= count:
+                variance(n - 1)
+            if n + 1 < count:
+                total = channel_sum(n + 1)
+            if n < count:
+                square(n, 0)
+            if n + 1 < count:
+                take_mean(n + 1, total)
+                products(n + 1)
+            if n < count:
+                square(n, 1)
+            if n >= LAG:
+                normalise(n - LAG)
+            if n > LAG:
+                store(n - LAG - 1)
+        store(count - 1)

@@ -20,10 +20,10 @@ P = 128
 HALF = 64
 CG = 4
 GROUPS = CM // CG
-RAW_BUFS = 6
-LAG = 2
-VECTOR_COLS_LATE = 16
-VECTOR_COLS_LAST = 64
+RAW_BUFS = 5
+VECTOR_COLS_EARLY = 16
+VECTOR_COLS_LATE = 32
+VECTOR_COLS_LAST = 80
 
 
 def tile_trianglemultiplication_pa_kernel(tc, left, right, ln_c_w, ln_c_b, out):
@@ -73,7 +73,7 @@ def tile_trianglemultiplication_pa_kernel(tc, left, right, ln_c_w, ln_c_b, out):
             codes[side, s] = keep.tile([P, CM * P], U32, name="codes_%s%d" % (side, s), align_bytes=64)
             scales[side, s] = keep.tile([P, CM * P], U8, name="scales_%s%d" % (side, s), align_bytes=64)
 
-        raw, grouped = {}, {}
+        raw, sorted_words, grouped = {}, {}, {}
         t_banks, mean, centred, squares, rstd_t, rstd_bank, result = {}, {}, {}, {}, {}, {}, {}
 
         def load(n_half):
@@ -86,16 +86,30 @@ def tile_trianglemultiplication_pa_kernel(tc, left, right, ln_c_w, ln_c_b, out):
             for e in range(2):
                 nc.sync.dma_start(out=tile[e:P:2, :].rearrange("p (g r) -> p g r", r=16 * CM), in_=rows[e])
 
+        def sort_words(n_sort, copies):
+            n_half, part = divmod(n_sort, 2)
+            words = raw[n_half][:].bitcast(F32).rearrange("q (p u w) -> q u p w", u=2, w=CM // 2)
+            tile = work.tile([P, CG, 2, P], F32, name="sorted_words", bufs=4)
+            sorted_words[n_sort] = tile
+            for u in range(2):
+                copies[u](
+                    out=tile[:, :, u, :].rearrange("q w p -> q p w"),
+                    in_=words[:, u, :, CG * part : CG * (part + 1)],
+                )
+            if part == 1 and n_half + RAW_BUFS < len(halves):
+                load(n_half + RAW_BUFS)
+
         def fill(n_fill):
             chunk, h, g = fills[n_fill]
-            n_half = n_fill // GROUPS
+            values = sorted_words[n_fill // 2][:].rearrange("q w u p -> q (w u p)").bitcast(BF16)
             bank = psum.tile([P, CG * 2 * P], BF16, name="turned", tag="aux", bufs=3)
             for c in range(CG):
                 for u in range(2):
-                    first = CM * u + CG * g + c
+                    word, low = divmod(CG * (g % 2) + c, 2)
+                    run = 2 * P * (2 * word + u)
                     slot = 2 * c + u
                     nc.tensor.transpose(
-                        bank[:, slot * P : (slot + 1) * P], raw[n_half][:, first : NK * CM // 2 : 2 * CM], ident_bf[:]
+                        bank[:, slot * P : (slot + 1) * P], values[:, run + low : run + 2 * P : 2], ident_bf[:]
                     )
             if h == 0:
                 grouped[chunk, g] = work.tile([P, CG * P * 4], BF16, name="grouped", bufs=5, align_bytes=64)
@@ -104,8 +118,6 @@ def tile_trianglemultiplication_pa_kernel(tc, left, right, ln_c_w, ln_c_b, out):
                 out=words[:, :, h * HALF : (h + 1) * HALF, :],
                 in_=bank[:].bitcast(F32).rearrange("p (c u m) -> p c m u", c=CG, u=2),
             )
-            if g == GROUPS - 1 and n_half + RAW_BUFS < len(halves):
-                load(n_half + RAW_BUFS)
 
         def quantize(n_fill):
             chunk, h, g = fills[n_fill]
@@ -148,7 +160,7 @@ def tile_trianglemultiplication_pa_kernel(tc, left, right, ln_c_w, ln_c_b, out):
                     product(n, CG * g + c, bank[:, c, :], True, True)
 
         def centre(n):
-            centred[n] = work.tile([P, CM, P], F32, name="centred", bufs=LAG + 2)
+            centred[n] = work.tile([P, CM, P], F32, name="centred", bufs=4)
             mu = mean[n][:].unsqueeze(1).to_broadcast([P, CG, P])
             for g in range(GROUPS):
                 nc.vector.tensor_tensor(
@@ -171,16 +183,15 @@ def tile_trianglemultiplication_pa_kernel(tc, left, right, ln_c_w, ln_c_b, out):
             nc.scalar.activation(out=rstd_t[n][:], in_=sums[:], func=ACT.Abs_reciprocal_sqrt, scale=1.0 / CM, bias=EPS)
 
         def vector_cols(n):
-            if n >= len(units) - LAG:
+            if n == len(units) - 1:
                 return VECTOR_COLS_LAST
-            return VECTOR_COLS_LATE if n + LAG > last_fill_period else 0
+            return VECTOR_COLS_LATE if n >= last_fill_period else VECTOR_COLS_EARLY
 
         def turn_rstd(n):
             bank = psum.tile([P, P + CM], F32, name="rstd_bank")
             rstd_bank[n] = bank
             nc.tensor.transpose(bank[:, 0:P], rstd_t[n][:], ident_f32[:])
-            if vector_cols(n):
-                nc.tensor.matmul(bank[:, P : P + CM], lhsT=ident_bf[:], rhs=bias_bf[:], start=True, stop=True)
+            nc.tensor.matmul(bank[:, P : P + CM], lhsT=ident_bf[:], rhs=bias_bf[:], start=True, stop=True)
 
         def add_bias(engine, n, g, j0, j1, row):
             cs = slice(CG * g, CG * (g + 1))
@@ -205,9 +216,8 @@ def tile_trianglemultiplication_pa_kernel(tc, left, right, ln_c_w, ln_c_b, out):
                         op1=ALU.mult,
                     )
                 add_bias(nc.gpsimd, n, g, 0, split, bias)
-            if split < P:
-                for g in range(GROUPS):
-                    add_bias(nc.vector, n, g, split, P, rstd_bank[n][:, P : P + CM])
+            for g in range(GROUPS):
+                add_bias(nc.vector, n, g, split, P, rstd_bank[n][:, P : P + CM])
 
         def store(n):
             a, b = units[n]
@@ -219,29 +229,39 @@ def tile_trianglemultiplication_pa_kernel(tc, left, right, ln_c_w, ln_c_b, out):
         nc.sync.dma_start(out=bias_bf[:], in_=ln_c_b.partition_broadcast(P))
 
         done = 2 * per_chunk
-        for n_fill in range(done):
-            fill(n_fill)
-            quantize(n_fill)
+        on_vector = (nc.vector.tensor_copy, nc.vector.tensor_copy)
+        sort_words(0, on_vector)
+        for n_sort in range(done // 2):
+            if n_sort + 1 < done // 2:
+                sort_words(n_sort + 1, on_vector)
+            for n_fill in (2 * n_sort, 2 * n_sort + 1):
+                fill(n_fill)
+                quantize(n_fill)
         nc.vector.tensor_copy(out=gain[:], in_=gain_bf[:])
         nc.vector.tensor_copy(out=bias[:], in_=bias_bf[:])
         total = channel_sum(0)
         take_mean(0, total)
         products(0)
+        sorts_done = done // 2
+
+        for n_sort in range(sorts_done, fills_by[0] // 2):
+            sort_words(n_sort, on_vector)
+        sorts_done = fills_by[0] // 2
 
         count = len(units)
-        for n in range(count + LAG):
-            if n >= LAG:
-                turn_rstd(n - LAG)
+        for n in range(count + 1):
             if n < count:
                 centre(n)
+            if n >= 1:
+                variance(n - 1)
             todo = range(done, fills_by.get(n, done))
             for n_fill in todo:
                 fill(n_fill)
+            if n >= 1:
+                turn_rstd(n - 1)
             for n_fill in todo:
                 quantize(n_fill)
             done += len(todo)
-            if 1 <= n <= count:
-                variance(n - 1)
             if n + 1 < count:
                 total = channel_sum(n + 1)
             if n < count:
@@ -251,8 +271,15 @@ def tile_trianglemultiplication_pa_kernel(tc, left, right, ln_c_w, ln_c_b, out):
                 products(n + 1)
             if n < count:
                 square(n, 1)
-            if n >= LAG:
-                normalise(n - LAG)
-            if n > LAG:
-                store(n - LAG - 1)
+            if n >= 1:
+                normalise(n - 1)
+            ahead = range(sorts_done, -(-fills_by.get(n + 1, len(fills)) // 2))
+            sorts_done += len(ahead)
+            next_fills = fills_by.get(n + 1, done) - done
+            for n_sort in ahead:
+                first = nc.vector.tensor_copy if next_fills > GROUPS else nc.scalar.copy
+                second = nc.vector.tensor_copy if next_fills >= GROUPS else nc.scalar.copy
+                sort_words(n_sort, (first, second))
+            if n >= 2:
+                store(n - 2)
         store(count - 1)

@@ -21,9 +21,7 @@ HALF = 64
 CG = 4
 GROUPS = CM // CG
 RAW_BUFS = 5
-VECTOR_COLS_EARLY = 16
-VECTOR_COLS_LATE = 32
-VECTOR_COLS_LAST = 80
+VECTOR_COLS = 32
 
 
 def tile_trianglemultiplication_pa_kernel(tc, left, right, ln_c_w, ln_c_b, out):
@@ -32,26 +30,19 @@ def tile_trianglemultiplication_pa_kernel(tc, left, right, ln_c_w, ln_c_b, out):
 
     chunks = [("left", 0), ("right", 0)]
     units = [(0, 0)]
-    first_unit = {}
     for s in range(1, tiles):
         chunks.append(("right", s))
-        first_unit[("right", s)] = len(units)
         units.extend((a, s) for a in range(s))
         chunks.append(("left", s))
-        first_unit[("left", s)] = len(units)
         units.extend((s, b) for b in range(s + 1))
     halves = [(chunk, h) for chunk in chunks for h in range(2)]
     fills = [(chunk, h, g) for chunk, h in halves for g in range(GROUPS)]
     per_chunk = 2 * GROUPS
 
-    fills_by = {}
-    start = 0
-    for n_chunk in range(2, len(chunks)):
-        end = first_unit[chunks[n_chunk]]
-        for n in range(start, end):
-            fills_by[n] = n_chunk * per_chunk + -(-per_chunk * (n + 1 - start) // (end - start))
-        start = end
-    last_fill_period = start - 1
+    count = len(units)
+
+    def fills_by(n):
+        return min(len(fills), per_chunk * (3 + min(n, 1)) + GROUPS * max(n - 1, 0))
 
     with ExitStack() as ctx:
         keep = ctx.enter_context(tc.tile_pool(name="keep", bufs=1))
@@ -74,7 +65,10 @@ def tile_trianglemultiplication_pa_kernel(tc, left, right, ln_c_w, ln_c_b, out):
             scales[side, s] = keep.tile([P, CM * P], U8, name="scales_%s%d" % (side, s), align_bytes=64)
 
         raw, sorted_words, grouped = {}, {}, {}
-        t_banks, mean, centred, squares, rstd_t, rstd_bank, result = {}, {}, {}, {}, {}, {}, {}
+        t_banks, mean, centred, squares, rstd_t, result = {}, {}, {}, {}, {}, {}
+        rstd_bank = psum.tile([P, P + CM], F32, name="rstd_bank")
+        rstd = rstd_bank[:, 0:P]
+        bias_psum = rstd_bank[:, P : P + CM]
 
         def load(n_half):
             (side, s), h = halves[n_half]
@@ -89,7 +83,7 @@ def tile_trianglemultiplication_pa_kernel(tc, left, right, ln_c_w, ln_c_b, out):
         def sort_words(n_sort, copies):
             n_half, part = divmod(n_sort, 2)
             words = raw[n_half][:].bitcast(F32).rearrange("q (p u w) -> q u p w", u=2, w=CM // 2)
-            tile = work.tile([P, CG, 2, P], F32, name="sorted_words", bufs=4)
+            tile = work.tile([P, CG, 2, P], F32, name="sorted_words", bufs=5)
             sorted_words[n_sort] = tile
             for u in range(2):
                 copies[u](
@@ -182,16 +176,8 @@ def tile_trianglemultiplication_pa_kernel(tc, left, right, ln_c_w, ln_c_b, out):
             rstd_t[n] = work.tile([P, P], F32, name="rstd_t")
             nc.scalar.activation(out=rstd_t[n][:], in_=sums[:], func=ACT.Abs_reciprocal_sqrt, scale=1.0 / CM, bias=EPS)
 
-        def vector_cols(n):
-            if n == len(units) - 1:
-                return VECTOR_COLS_LAST
-            return VECTOR_COLS_LATE if n >= last_fill_period else VECTOR_COLS_EARLY
-
         def turn_rstd(n):
-            bank = psum.tile([P, P + CM], F32, name="rstd_bank")
-            rstd_bank[n] = bank
-            nc.tensor.transpose(bank[:, 0:P], rstd_t[n][:], ident_f32[:])
-            nc.tensor.matmul(bank[:, P : P + CM], lhsT=ident_bf[:], rhs=bias_bf[:], start=True, stop=True)
+            nc.tensor.transpose(rstd, rstd_t[n][:], ident_f32[:])
 
         def add_bias(engine, n, g, j0, j1, row):
             cs = slice(CG * g, CG * (g + 1))
@@ -202,22 +188,32 @@ def tile_trianglemultiplication_pa_kernel(tc, left, right, ln_c_w, ln_c_b, out):
                 op=ALU.add,
             )
 
-        def normalise(n):
+        def normalise(n, scalar_groups, vector_cols):
             result[n] = work.tile([P, P, CM], F32, name="result", bufs=3)
-            split = P - vector_cols(n)
-            for g in range(GROUPS):
+            split = P - vector_cols
+            for g in range(scalar_groups):
+                cs = slice(CG * g, CG * (g + 1))
+                part = centred[n][:, cs, :]
+                nc.vector.tensor_tensor(
+                    out=part, in0=part, in1=rstd.unsqueeze(1).to_broadcast([P, CG, P]), op=ALU.mult
+                )
                 for c in range(CG * g, CG * (g + 1)):
-                    nc.vector.scalar_tensor_tensor(
-                        out=centred[n][:, c, :],
-                        in0=centred[n][:, c, :],
-                        scalar=gain[:, c : c + 1],
-                        in1=rstd_bank[n][:, 0:P],
-                        op0=ALU.mult,
-                        op1=ALU.mult,
+                    row = centred[n][:, c, :]
+                    nc.scalar.activation(
+                        out=row, in_=row, func=ACT.Identity, scale=gain[:, c : c + 1], bias=bias[:, c : c + 1]
                     )
-                add_bias(nc.gpsimd, n, g, 0, split, bias)
-            for g in range(GROUPS):
-                add_bias(nc.vector, n, g, split, P, rstd_bank[n][:, P : P + CM])
+                nc.scalar.copy(out=result[n][:, :, cs], in_=part.rearrange("p c j -> p j c"))
+            for g in range(scalar_groups, GROUPS):
+                for c in range(CG * g, CG * (g + 1)):
+                    row = centred[n][:, c, :]
+                    nc.vector.scalar_tensor_tensor(
+                        out=row, in0=row, scalar=gain[:, c : c + 1], in1=rstd, op0=ALU.mult, op1=ALU.mult
+                    )
+                if split:
+                    add_bias(nc.gpsimd, n, g, 0, split, bias)
+            if vector_cols:
+                for g in range(scalar_groups, GROUPS):
+                    add_bias(nc.vector, n, g, split, P, bias_psum)
 
         def store(n):
             a, b = units[n]
@@ -242,44 +238,49 @@ def tile_trianglemultiplication_pa_kernel(tc, left, right, ln_c_w, ln_c_b, out):
         total = channel_sum(0)
         take_mean(0, total)
         products(0)
-        sorts_done = done // 2
-
-        for n_sort in range(sorts_done, fills_by[0] // 2):
+        nc.tensor.matmul(bias_psum, lhsT=ident_bf[:], rhs=bias_bf[:], start=True, stop=True)
+        for n_sort in range(done // 2, fills_by(0) // 2):
             sort_words(n_sort, on_vector)
-        sorts_done = fills_by[0] // 2
 
-        count = len(units)
+        on_scalar = (nc.scalar.copy, nc.scalar.copy)
         for n in range(count + 1):
+            todo = range(done, fills_by(n))
+            done = fills_by(n)
+            ahead = range(done // 2, fills_by(n + 1) // 2)
+            if n >= 1:
+                for n_sort in ahead[:1]:
+                    sort_words(n_sort, on_scalar)
             if n < count:
                 centre(n)
             if n >= 1:
                 variance(n - 1)
-            todo = range(done, fills_by.get(n, done))
             for n_fill in todo:
                 fill(n_fill)
             if n >= 1:
                 turn_rstd(n - 1)
             for n_fill in todo:
                 quantize(n_fill)
-            done += len(todo)
+            if n == 0:
+                for n_sort in ahead:
+                    sort_words(n_sort, on_vector)
             if n + 1 < count:
                 total = channel_sum(n + 1)
             if n < count:
                 square(n, 0)
+                square(n, 1)
             if n + 1 < count:
                 take_mean(n + 1, total)
                 products(n + 1)
-            if n < count:
-                square(n, 1)
             if n >= 1:
-                normalise(n - 1)
-            ahead = range(sorts_done, -(-fills_by.get(n + 1, len(fills)) // 2))
-            sorts_done += len(ahead)
-            next_fills = fills_by.get(n + 1, done) - done
-            for n_sort in ahead:
-                first = nc.vector.tensor_copy if next_fills > GROUPS else nc.scalar.copy
-                second = nc.vector.tensor_copy if next_fills >= GROUPS else nc.scalar.copy
-                sort_words(n_sort, (first, second))
+                for n_sort in ahead[1:]:
+                    sort_words(n_sort, on_scalar)
+            if n == count:
+                normalise(n - 1, 2, P)
+            elif n >= 1:
+                if len(todo):
+                    normalise(n - 1, 0, VECTOR_COLS)
+                else:
+                    normalise(n - 1, 1, 0)
             if n >= 2:
                 store(n - 2)
         store(count - 1)

@@ -21,7 +21,7 @@ HALF = 64
 CG = 4
 GROUPS = CM // CG
 RAW_BUFS = 5
-VECTOR_COLS = 32
+VECTOR_COLS = 24
 
 
 def tile_trianglemultiplication_pa_kernel(tc, left, right, ln_c_w, ln_c_b, out):
@@ -42,7 +42,7 @@ def tile_trianglemultiplication_pa_kernel(tc, left, right, ln_c_w, ln_c_b, out):
     count = len(units)
 
     def fills_by(n):
-        return min(len(fills), per_chunk * (3 + min(n, 1)) + GROUPS * max(n - 1, 0))
+        return min(len(fills), per_chunk * (3 + min(n + 1, 1)) + GROUPS * max(n, 0))
 
     with ExitStack() as ctx:
         keep = ctx.enter_context(tc.tile_pool(name="keep", bufs=1))
@@ -64,7 +64,7 @@ def tile_trianglemultiplication_pa_kernel(tc, left, right, ln_c_w, ln_c_b, out):
             codes[side, s] = keep.tile([P, CM * P], U32, name="codes_%s%d" % (side, s), align_bytes=64)
             scales[side, s] = keep.tile([P, CM * P], U8, name="scales_%s%d" % (side, s), align_bytes=64)
 
-        raw, sorted_words, grouped = {}, {}, {}
+        raw, sorted_words, grouped, total, sums = {}, {}, {}, {}, {}
         t_banks, mean, centred, squares, rstd_t, result = {}, {}, {}, {}, {}, {}
         rstd_bank = psum.tile([P, P + CM], F32, name="rstd_bank")
         rstd = rstd_bank[:, 0:P]
@@ -80,16 +80,23 @@ def tile_trianglemultiplication_pa_kernel(tc, left, right, ln_c_w, ln_c_b, out):
             for e in range(2):
                 nc.sync.dma_start(out=tile[e:P:2, :].rearrange("p (g r) -> p g r", r=16 * CM), in_=rows[e])
 
-        def sort_words(n_sort, copies):
+        def sort_words(n_sort, u, copy):
             n_half, part = divmod(n_sort, 2)
             words = raw[n_half][:].bitcast(F32).rearrange("q (p u w) -> q u p w", u=2, w=CM // 2)
-            tile = work.tile([P, CG, 2, P], F32, name="sorted_words", bufs=5)
-            sorted_words[n_sort] = tile
+            if n_sort not in sorted_words:
+                sorted_words[n_sort] = work.tile([P, CG, 2, P], F32, name="sorted_words", bufs=5)
+            copy(
+                out=sorted_words[n_sort][:, :, u, :].rearrange("q w p -> q p w"),
+                in_=words[:, u, :, CG * part : CG * (part + 1)],
+            )
+
+        def sort_on_vector(n_sort):
             for u in range(2):
-                copies[u](
-                    out=tile[:, :, u, :].rearrange("q w p -> q p w"),
-                    in_=words[:, u, :, CG * part : CG * (part + 1)],
-                )
+                sort_words(n_sort, u, nc.vector.tensor_copy)
+            load_after(n_sort)
+
+        def load_after(n_sort):
+            n_half, part = divmod(n_sort, 2)
             if part == 1 and n_half + RAW_BUFS < len(halves):
                 load(n_half + RAW_BUFS)
 
@@ -136,18 +143,17 @@ def tile_trianglemultiplication_pa_kernel(tc, left, right, ln_c_w, ln_c_b, out):
                 stop=stop,
             )
 
-        def channel_sum(n):
-            total = psum.tile([P, P], F32, name="total", tag="aux", bufs=3)
-            for c in range(CM):
-                product(n, c, total[:], c == 0, c == CM - 1)
-            return total
+        def channel_sum(n, part):
+            if part == 0:
+                total[n] = psum.tile([P, P], F32, name="total", tag="aux", bufs=3)
+            for c in range(part * CM // 2, (part + 1) * CM // 2):
+                product(n, c, total[n][:], c == 0, c == CM - 1)
+            if part == 1:
+                mean[n] = work.tile([P, P], F32, name="mean")
+                nc.scalar.activation(out=mean[n][:], in_=total[n][:], func=ACT.Copy, scale=1.0 / CM)
 
-        def take_mean(n, total):
-            mean[n] = work.tile([P, P], F32, name="mean")
-            nc.scalar.activation(out=mean[n][:], in_=total[:], func=ACT.Copy, scale=1.0 / CM)
-
-        def products(n):
-            for g in range(GROUPS):
+        def products(n, part):
+            for g in range(part * GROUPS // 2, (part + 1) * GROUPS // 2):
                 bank = psum.tile([P, CG, P], F32, name="t_bank", bufs=GROUPS)
                 t_banks[n, g] = bank
                 for c in range(CG):
@@ -167,14 +173,23 @@ def tile_trianglemultiplication_pa_kernel(tc, left, right, ln_c_w, ln_c_b, out):
             cs = slice(part * CM // 2, (part + 1) * CM // 2)
             nc.scalar.activation(out=squares[n][:, cs, :], in_=centred[n][:, cs, :], func=ACT.Square)
 
-        def variance(n):
-            sums = psum.tile([P, P], F32, name="sums", tag="aux", bufs=3)
-            for c in range(CM):
+        def variance(n, part):
+            if part == 0:
+                sums[n] = psum.tile([P, P], F32, name="sums", tag="aux", bufs=3)
+            for c in range(part * CM // 2, (part + 1) * CM // 2):
                 nc.tensor.matmul(
-                    sums[:], lhsT=squares[n][:, c, :], rhs=ident_f32[:], start=c == 0, stop=c == CM - 1, is_transpose=True
+                    sums[n][:],
+                    lhsT=squares[n][:, c, :],
+                    rhs=ident_f32[:],
+                    start=c == 0,
+                    stop=c == CM - 1,
+                    is_transpose=True,
                 )
-            rstd_t[n] = work.tile([P, P], F32, name="rstd_t")
-            nc.scalar.activation(out=rstd_t[n][:], in_=sums[:], func=ACT.Abs_reciprocal_sqrt, scale=1.0 / CM, bias=EPS)
+            if part == 1:
+                rstd_t[n] = work.tile([P, P], F32, name="rstd_t")
+                nc.scalar.activation(
+                    out=rstd_t[n][:], in_=sums[n][:], func=ACT.Abs_reciprocal_sqrt, scale=1.0 / CM, bias=EPS
+                )
 
         def turn_rstd(n):
             nc.tensor.transpose(rstd, rstd_t[n][:], ident_f32[:])
@@ -225,55 +240,51 @@ def tile_trianglemultiplication_pa_kernel(tc, left, right, ln_c_w, ln_c_b, out):
         nc.sync.dma_start(out=bias_bf[:], in_=ln_c_b.partition_broadcast(P))
 
         done = 2 * per_chunk
-        on_vector = (nc.vector.tensor_copy, nc.vector.tensor_copy)
-        sort_words(0, on_vector)
+        sort_on_vector(0)
         for n_sort in range(done // 2):
             if n_sort + 1 < done // 2:
-                sort_words(n_sort + 1, on_vector)
+                sort_on_vector(n_sort + 1)
             for n_fill in (2 * n_sort, 2 * n_sort + 1):
                 fill(n_fill)
                 quantize(n_fill)
         nc.vector.tensor_copy(out=gain[:], in_=gain_bf[:])
         nc.vector.tensor_copy(out=bias[:], in_=bias_bf[:])
-        total = channel_sum(0)
-        take_mean(0, total)
-        products(0)
         nc.tensor.matmul(bias_psum, lhsT=ident_bf[:], rhs=bias_bf[:], start=True, stop=True)
-        for n_sort in range(done // 2, fills_by(0) // 2):
-            sort_words(n_sort, on_vector)
+        for n_sort in range(done // 2, fills_by(-1) // 2):
+            sort_on_vector(n_sort)
 
-        on_scalar = (nc.scalar.copy, nc.scalar.copy)
-        for n in range(count + 1):
+        for n in range(-1, count + 1):
             todo = range(done, fills_by(n))
             done = fills_by(n)
             ahead = range(done // 2, fills_by(n + 1) // 2)
-            if n >= 1:
-                for n_sort in ahead[:1]:
-                    sort_words(n_sort, on_scalar)
-            if n < count:
+            if 0 <= n < count:
                 centre(n)
-            if n >= 1:
-                variance(n - 1)
-            for n_fill in todo:
-                fill(n_fill)
-            if n >= 1:
-                turn_rstd(n - 1)
+            for part in range(2):
+                if n >= 1:
+                    variance(n - 1, part)
+                if n + 1 < count:
+                    channel_sum(n + 1, part)
+            for part in range(2):
+                if n >= 0 and part == 0 and len(ahead):
+                    sort_words(ahead[0], 0, nc.scalar.copy)
+                for n_fill in todo[part * len(todo) // 2 : (part + 1) * len(todo) // 2]:
+                    fill(n_fill)
+                if n >= 1 and part == 0:
+                    turn_rstd(n - 1)
+                if n + 1 < count:
+                    products(n + 1, part)
+                if 0 <= n < count:
+                    square(n, part)
+            for n_sort in ahead:
+                if n < 0:
+                    sort_on_vector(n_sort)
+                else:
+                    sort_words(n_sort, 1, nc.vector.tensor_copy)
+            if n >= 0 and len(ahead):
+                sort_words(ahead[1], 0, nc.scalar.copy)
+                load_after(ahead[1])
             for n_fill in todo:
                 quantize(n_fill)
-            if n == 0:
-                for n_sort in ahead:
-                    sort_words(n_sort, on_vector)
-            if n + 1 < count:
-                total = channel_sum(n + 1)
-            if n < count:
-                square(n, 0)
-                square(n, 1)
-            if n + 1 < count:
-                take_mean(n + 1, total)
-                products(n + 1)
-            if n >= 1:
-                for n_sort in ahead[1:]:
-                    sort_words(n_sort, on_scalar)
             if n == count:
                 normalise(n - 1, 2, P)
             elif n >= 1:

from contextlib import ExitStack

import concourse.mybir as mybir
from concourse.masks import make_identity

NI, NJ, NK, CM = 512, 512, 512, 16
EPS = 1e-5
FLOPS = 2 * NI * NJ * NK * CM

F32 = mybir.dt.float32
BF16 = mybir.dt.bfloat16
U32 = mybir.dt.uint32
U8 = mybir.dt.uint8
E5M2 = mybir.dt.float8_e5m2_x4
E4M3 = mybir.dt.float8_e4m3fn_x4
ALU = mybir.AluOpType
ACT = mybir.ActivationFunctionType

P = 128
HALF = 64
CG = 4
GROUPS = CM // CG
RAW_BUFS = 5
VECTOR_COLS = 24


def tile_trianglemultiplication_pa_kernel(tc, left, right, ln_c_w, ln_c_b, out):
    nc = tc.nc
    tiles = NI // P

    chunks = [("left", 0), ("right", 0)]
    units = [(0, 0)]
    for s in range(1, tiles):
        chunks.append(("right", s))
        units.extend((a, s) for a in range(s))
        chunks.append(("left", s))
        units.extend((s, b) for b in range(s + 1))
    halves = [(chunk, h) for chunk in chunks for h in range(2)]
    fills = [(chunk, h, g) for chunk, h in halves for g in range(GROUPS)]
    per_chunk = 2 * GROUPS

    count = len(units)

    def fills_by(n):
        return min(len(fills), per_chunk * (3 + min(n + 1, 1)) + GROUPS * max(n, 0))

    with ExitStack() as ctx:
        keep = ctx.enter_context(tc.tile_pool(name="keep", bufs=1))
        work = ctx.enter_context(tc.tile_pool(name="work", bufs=2))
        psum = ctx.enter_context(tc.psum_pool(name="psum", bufs=1))
        ctx.enter_context(tc.manual_schedule())

        ident_bf = keep.tile([P, P], BF16, name="ident_bf")
        ident_f32 = keep.tile([P, P], F32, name="ident_f32")
        make_identity(nc, ident_bf[:])
        make_identity(nc, ident_f32[:])
        gain_bf = keep.tile([P, CM], BF16, name="gain_bf")
        bias_bf = keep.tile([P, CM], BF16, name="bias_bf")
        gain = keep.tile([P, CM], F32, name="gain")
        bias = keep.tile([P, CM], F32, name="bias")

        codes, scales = {}, {}
        for side, s in chunks:
            codes[side, s] = keep.tile([P, CM * P], U32, name="codes_%s%d" % (side, s), align_bytes=64)
            scales[side, s] = keep.tile([P, CM * P], U8, name="scales_%s%d" % (side, s), align_bytes=64)

        raw, sorted_words, grouped, total, sums = {}, {}, {}, {}, {}
        t_banks, mean, centred, squares, rstd_t, result = {}, {}, {}, {}, {}, {}
        rstd_bank = psum.tile([P, P + CM], F32, name="rstd_bank")
        rstd = rstd_bank[:, 0:P]
        bias_psum = rstd_bank[:, P : P + CM]

        def load(n_half):
            (side, s), h = halves[n_half]
            src = left if side == "left" else right
            row0 = s * P + h * HALF
            rows = src[row0 : row0 + HALF].rearrange("i (g e r) c -> e i g (r c)", e=2, r=16)
            tile = work.tile([P, NK * CM // 2], BF16, name="raw", bufs=RAW_BUFS)
            raw[n_half] = tile
            for e in range(2):
                nc.sync.dma_start(out=tile[e:P:2, :].rearrange("p (g r) -> p g r", r=16 * CM), in_=rows[e])

        def sort_words(n_sort, u, copy):
            n_half, part = divmod(n_sort, 2)
            words = raw[n_half][:].bitcast(F32).rearrange("q (p u w) -> q u p w", u=2, w=CM // 2)
            if n_sort not in sorted_words:
                sorted_words[n_sort] = work.tile([P, CG, 2, P], F32, name="sorted_words", bufs=5)
            copy(
                out=sorted_words[n_sort][:, :, u, :].rearrange("q w p -> q p w"),
                in_=words[:, u, :, CG * part : CG * (part + 1)],
            )

        def sort_on_vector(n_sort):
            for u in range(2):
                sort_words(n_sort, u, nc.vector.tensor_copy)
            load_after(n_sort)

        def load_after(n_sort):
            n_half, part = divmod(n_sort, 2)
            if part == 1 and n_half + RAW_BUFS < len(halves):
                load(n_half + RAW_BUFS)

        def fill(n_fill):
            chunk, h, g = fills[n_fill]
            values = sorted_words[n_fill // 2][:].rearrange("q w u p -> q (w u p)").bitcast(BF16)
            bank = psum.tile([P, CG * 2 * P], BF16, name="turned", tag="aux", bufs=3)
            for c in range(CG):
                for u in range(2):
                    word, low = divmod(CG * (g % 2) + c, 2)
                    run = 2 * P * (2 * word + u)
                    slot = 2 * c + u
                    nc.tensor.transpose(
                        bank[:, slot * P : (slot + 1) * P], values[:, run + low : run + 2 * P : 2], ident_bf[:]
                    )
            if h == 0:
                grouped[chunk, g] = work.tile([P, CG * P * 4], BF16, name="grouped", bufs=5, align_bytes=64)
            words = grouped[chunk, g][:].bitcast(F32).rearrange("p (c m u) -> p c m u", c=CG, u=2)
            nc.scalar.copy(
                out=words[:, :, h * HALF : (h + 1) * HALF, :],
                in_=bank[:].bitcast(F32).rearrange("p (c u m) -> p c m u", c=CG, u=2),
            )

        def quantize(n_fill):
            chunk, h, g = fills[n_fill]
            if h == 1:
                cols = slice(g * CG * P, (g + 1) * CG * P)
                nc.vector.quantize_mx(
                    out=codes[chunk][:, cols].bitcast(E5M2 if chunk[0] == "left" else E4M3),
                    scales=scales[chunk][:, cols],
                    in_=grouped[chunk, g][:],
                )

        def product(n, c, dst, start, stop):
            a, b = units[n]
            cols = slice(c * P, (c + 1) * P)
            nc.tensor.matmul_mx(
                out=dst,
                lhsT=codes["left", a][:, cols].bitcast(E5M2),
                lhsT_scale=scales["left", a][:, cols],
                rhs=codes["right", b][:, cols].bitcast(E4M3),
                rhs_scale=scales["right", b][:, cols],
                start=start,
                stop=stop,
            )

        def channel_sum(n, part):
            if part == 0:
                total[n] = psum.tile([P, P], F32, name="total", tag="aux", bufs=3)
            for c in range(part * CM // 2, (part + 1) * CM // 2):
                product(n, c, total[n][:], c == 0, c == CM - 1)
            if part == 1:
                mean[n] = work.tile([P, P], F32, name="mean")
                nc.scalar.activation(out=mean[n][:], in_=total[n][:], func=ACT.Copy, scale=1.0 / CM)

        def products(n, part):
            for g in range(part * GROUPS // 2, (part + 1) * GROUPS // 2):
                bank = psum.tile([P, CG, P], F32, name="t_bank", bufs=GROUPS)
                t_banks[n, g] = bank
                for c in range(CG):
                    product(n, CG * g + c, bank[:, c, :], True, True)

        def centre(n):
            centred[n] = work.tile([P, CM, P], F32, name="centred", bufs=4)
            mu = mean[n][:].unsqueeze(1).to_broadcast([P, CG, P])
            for g in range(GROUPS):
                nc.vector.tensor_tensor(
                    out=centred[n][:, CG * g : CG * (g + 1), :], in0=t_banks[n, g][:], in1=mu, op=ALU.subtract
                )

        def square(n, part):
            if part == 0:
                squares[n] = work.tile([P, CM, P], F32, name="squares")
            cs = slice(part * CM // 2, (part + 1) * CM // 2)
            nc.scalar.activation(out=squares[n][:, cs, :], in_=centred[n][:, cs, :], func=ACT.Square)

        def variance(n, part):
            if part == 0:
                sums[n] = psum.tile([P, P], F32, name="sums", tag="aux", bufs=3)
            for c in range(part * CM // 2, (part + 1) * CM // 2):
                nc.tensor.matmul(
                    sums[n][:],
                    lhsT=squares[n][:, c, :],
                    rhs=ident_f32[:],
                    start=c == 0,
                    stop=c == CM - 1,
                    is_transpose=True,
                )
            if part == 1:
                rstd_t[n] = work.tile([P, P], F32, name="rstd_t")
                nc.scalar.activation(
                    out=rstd_t[n][:], in_=sums[n][:], func=ACT.Abs_reciprocal_sqrt, scale=1.0 / CM, bias=EPS
                )

        def turn_rstd(n):
            nc.tensor.transpose(rstd, rstd_t[n][:], ident_f32[:])

        def add_bias(engine, n, g, j0, j1, row):
            cs = slice(CG * g, CG * (g + 1))
            engine.tensor_tensor(
                out=result[n][:, j0:j1, cs],
                in0=centred[n][:, cs, j0:j1].rearrange("p c j -> p j c"),
                in1=row[:, cs].unsqueeze(1).to_broadcast([P, j1 - j0, CG]),
                op=ALU.add,
            )

        def normalise(n, scalar_groups, vector_cols):
            result[n] = work.tile([P, P, CM], F32, name="result", bufs=3)
            split = P - vector_cols
            for g in range(scalar_groups):
                cs = slice(CG * g, CG * (g + 1))
                part = centred[n][:, cs, :]
                nc.vector.tensor_tensor(
                    out=part, in0=part, in1=rstd.unsqueeze(1).to_broadcast([P, CG, P]), op=ALU.mult
                )
                for c in range(CG * g, CG * (g + 1)):
                    row = centred[n][:, c, :]
                    nc.scalar.activation(
                        out=row, in_=row, func=ACT.Identity, scale=gain[:, c : c + 1], bias=bias[:, c : c + 1]
                    )
                nc.scalar.copy(out=result[n][:, :, cs], in_=part.rearrange("p c j -> p j c"))
            for g in range(scalar_groups, GROUPS):
                for c in range(CG * g, CG * (g + 1)):
                    row = centred[n][:, c, :]
                    nc.vector.scalar_tensor_tensor(
                        out=row, in0=row, scalar=gain[:, c : c + 1], in1=rstd, op0=ALU.mult, op1=ALU.mult
                    )
                if split:
                    add_bias(nc.gpsimd, n, g, 0, split, bias)
            if vector_cols:
                for g in range(scalar_groups, GROUPS):
                    add_bias(nc.vector, n, g, split, P, bias_psum)

        def store(n):
            a, b = units[n]
            nc.sync.dma_start(out=out[a * P : (a + 1) * P, b * P : (b + 1) * P, :], in_=result[n][:])

        for n_half in range(RAW_BUFS):
            load(n_half)
        nc.sync.dma_start(out=gain_bf[:], in_=ln_c_w.partition_broadcast(P))
        nc.sync.dma_start(out=bias_bf[:], in_=ln_c_b.partition_broadcast(P))

        done = 2 * per_chunk
        sort_on_vector(0)
        for n_sort in range(done // 2):
            if n_sort + 1 < done // 2:
                sort_on_vector(n_sort + 1)
            for n_fill in (2 * n_sort, 2 * n_sort + 1):
                fill(n_fill)
                quantize(n_fill)
        nc.vector.tensor_copy(out=gain[:], in_=gain_bf[:])
        nc.vector.tensor_copy(out=bias[:], in_=bias_bf[:])
        nc.tensor.matmul(bias_psum, lhsT=ident_bf[:], rhs=bias_bf[:], start=True, stop=True)
        for n_sort in range(done // 2, fills_by(-1) // 2):
            sort_on_vector(n_sort)

        for n in range(-1, count + 1):
            todo = range(done, fills_by(n))
            done = fills_by(n)
            ahead = range(done // 2, fills_by(n + 1) // 2)
            if 0 <= n < count:
                centre(n)
            for part in range(2):
                if n >= 1:
                    variance(n - 1, part)
                if n + 1 < count:
                    channel_sum(n + 1, part)
            for part in range(2):
                if n >= 0 and part == 0 and len(ahead):
                    sort_words(ahead[0], 0, nc.scalar.copy)
                for n_fill in todo[part * len(todo) // 2 : (part + 1) * len(todo) // 2]:
                    fill(n_fill)
                if n >= 1 and part == 0:
                    turn_rstd(n - 1)
                if n + 1 < count:
                    products(n + 1, part)
                if 0 <= n < count:
                    square(n, part)
            for n_sort in ahead:
                if n < 0:
                    sort_on_vector(n_sort)
                else:
                    sort_words(n_sort, 1, nc.vector.tensor_copy)
            if n >= 0 and len(ahead):
                sort_words(ahead[1], 0, nc.scalar.copy)
                load_after(ahead[1])
            for n_fill in todo:
                quantize(n_fill)
            if n == count:
                normalise(n - 1, 2, P)
            elif n >= 1:
                if len(todo):
                    normalise(n - 1, 0, VECTOR_COLS)
                else:
                    normalise(n - 1, 1, 0)
            if n >= 2:
                store(n - 2)
        store(count - 1)
